import numpy as np
import ml_dtypes


def mxq(x, axis, fmt="e4m3"):
    dtype, down = {"e4m3": (ml_dtypes.float8_e4m3fn, 7), "e5m2": (ml_dtypes.float8_e5m2, 14)}[fmt]
    v = np.moveaxis(np.asarray(x, np.float32).astype(ml_dtypes.bfloat16).astype(np.float64), axis, -1)
    blocks = v.reshape(v.shape[:-1] + (-1, 32))
    amax = np.abs(blocks).max(-1, keepdims=True)
    byte = np.maximum(np.where(amax > 0, np.frexp(amax)[1] - 1 + 127, 0) - down, 1)
    scale = np.exp2(byte - 127.0)
    codes = (blocks / scale).astype(np.float32).astype(dtype).astype(np.float64)
    return np.moveaxis((codes * scale).reshape(v.shape), -1, axis)


WIDE = False


def mx_kscale(k):
    if not WIDE:
        return np.ones(k)
    levels = np.array([10, -10, 5, -5, 0])
    if k % 512:
        return np.exp2(np.random.permutation(np.resize(levels, k // 32))).repeat(32)
    a = np.empty((k // 512, 16))
    for p in range(k // 512):
        a[p, :8] = np.random.permutation(np.resize(levels, 8))
        for g in range(8):
            far = levels[np.abs(levels - a[p, g]) >= 10]
            a[p, g + 8] = far[np.random.randint(len(far))]
    return np.exp2(a.ravel()).repeat(32)


BF16 = ml_dtypes.bfloat16


def bf(x):
    return np.asarray(x, np.float32).astype(BF16)


def f64(x):
    return np.asarray(x).astype(np.float64)


WAY, SHOT, QUERY_SHOT, D, M = 4, 6, 8, 640, 512
G, Q = 4, 5
NS, NQ = WAY * SHOT, WAY * QUERY_SHOT


def log_softmax(v, axis):
    z = v - v.max(axis, keepdims=True)
    return z - np.log(np.exp(z).sum(axis, keepdims=True))


def setup_inputs():
    s = mx_kscale(M)
    return {"feature_map": bf(np.random.standard_normal((NS + NQ, D, M)) * np.sqrt(M) * s),
            "weight2": bf(np.random.uniform(0.0, 1.0, (NS, NQ, M)) / s),
            "scale": bf(G * Q * Q * SHOT / np.sqrt(D) * (1.0 + 0.1 * np.random.standard_normal(1)))}


def reference(feature_map, weight2, scale):
    fq = mxq(f64(feature_map), 2, "e4m3")
    wq = mxq(f64(weight2), 2, "e4m3")
    support = fq[:NS]
    query = fq[NS:]
    centroid = (wq @ support.transpose(0, 2, 1)) / M
    query_r = (wq.transpose(1, 0, 2) @ query.transpose(0, 2, 1)).transpose(1, 0, 2) / M
    l2 = ((centroid - query_r) ** 2).sum(-1)
    neg_l2 = -l2.T
    logits = neg_l2 / (G * Q * Q * SHOT) * f64(scale)
    return log_softmax(logits, 1)

@@ -1,0 +1,372 @@
+from contextlib import ExitStack
+
+import concourse.mybir as mybir
+from concourse.masks import make_identity
+
+FLOPS = 2 * 2 * 24 * 32 * 640 * 512
+
+F32 = mybir.dt.float32
+BF16 = mybir.dt.bfloat16
+U32 = mybir.dt.uint32
+U8 = mybir.dt.uint8
+I32 = mybir.dt.int32
+FP8X4 = mybir.dt.float8_e4m3fn_x4
+ALU = mybir.AluOpType
+ACT = mybir.ActivationFunctionType
+AX = mybir.AxisListType
+
+P = 128
+NS = 24
+NQ = 32
+DC = 5
+X_BUFS = 14
+SLOT = 64
+LAG = 2
+BLK = 32
+LOGIT_FACTOR = -1.0 / (600.0 * 512.0 * 512.0)
+
+PIECES = {2: (8, 2), 1: (4, 1)}
+VECTOR_BANKS = {2: (4,), 1: (2,)}
+FULL_QUAD = ((2, 2),)
+QUERY_QUADS = (FULL_QUAD,) * 7 + (((2,), (1, 1)),)
+W2_SLOTS = (2, 3)
+
+
+def tile_proto_kernel(tc, feature_map, weight2, scale, out):
+    nc = tc.nc
+    loads = []
+    passes = []
+    images = []
+    for is_q, quads in ((False, (FULL_QUAD,) * (NS // 4)), (True, QUERY_QUADS)):
+        for t, quad in enumerate(quads):
+            h0 = 0
+            for group in quad:
+                members = []
+                for n in group:
+                    members.append(len(loads))
+                    loads.append((len(images), n))
+                    for il in range(n):
+                        images.append(4 * t + h0 + sum(loads[m][1] for m in members[:-1]) + il + (NS if is_q else 0))
+                total = sum(group)
+                passes.append((is_q, t, h0, total, members))
+                h0 += total
+    n_loads = len(loads)
+    runs = []
+    for x, entry in enumerate(passes):
+        ready = entry[4][-1] + LAG
+        if entry[3] == 4:
+            runs.append((x, 0, 2, 3, ready))
+            runs.append((x, 1, 2, 2, ready))
+        else:
+            runs.append((x, 0, 1, DC, ready))
+
+    with ExitStack() as ctx:
+        const = ctx.enter_context(tc.tile_pool(name="const", bufs=1))
+        xin = ctx.enter_context(tc.tile_pool(name="xin", bufs=X_BUFS))
+        gpool = ctx.enter_context(tc.tile_pool(name="gpool", bufs=4))
+        qpool = ctx.enter_context(tc.tile_pool(name="qpool", bufs=5))
+        tpool = ctx.enter_context(tc.psum_pool(name="tpool", bufs=6))
+        mpool = ctx.enter_context(tc.psum_pool(name="mpool", bufs=1))
+        jpool = ctx.enter_context(tc.tile_pool(name="jpool", bufs=2))
+        ctx.enter_context(tc.manual_schedule())
+
+        x_tiles = []
+
+        def load_next():
+            img = images[len(x_tiles)]
+            xt = xin.tile([P, DC * 512], BF16)
+            nc.sync.dma_start(out=xt[:], in_=feature_map[img].rearrange("(p c) m -> p (c m)", c=DC))
+            x_tiles.append(xt)
+
+        def copy_words(on_scalar, dst, src):
+            if on_scalar:
+                nc.scalar.copy(out=dst, in_=src)
+            else:
+                nc.vector.tensor_copy(out=dst, in_=src)
+
+        w_in = const.tile([P, 6, 512], BF16)
+        nc.sync.dma_start(
+            out=w_in[:],
+            in_=weight2.rearrange("s q m -> (s q) m").rearrange("(j p) m -> p j m", p=P),
+        )
+        sc_bf = const.tile([P, 1], BF16)
+        for k in range(X_BUFS):
+            load_next()
+
+        ident = const.tile([P, P], F32)
+        make_identity(nc, ident[:])
+        diffs = []
+        for r in range(3):
+            dt_r = const.tile([P, DC * P], F32, name="diff%d" % r)
+            nc.gpsimd.memset(dt_r[:], 0.0)
+            diffs.append(dt_r)
+
+        warm = const.tile([P, 1], F32)
+        nc.vector.memset(warm[:], 0.0)
+        nc.scalar.activation(out=warm[:], in_=warm[:], func=ACT.Exp)
+
+        w1c = const.tile([P, (NS + 1) * SLOT], U32, align_bytes=64)
+        w1s = const.tile([P, (NS + 1) * SLOT], U8, align_bytes=64)
+        w2c = const.tile([P, (NQ + 1) * SLOT], U32, align_bytes=64)
+        w2s = const.tile([P, (NQ + 1) * SLOT], U8, align_bytes=64)
+        c_sb = const.tile([P, DC * NQ * NS], F32)
+        l2_sb = const.tile([P, P], F32)
+        acc = const.tile([P, 2, 8], F32)
+        sc_f = const.tile([P, 1], F32)
+        cv = c_sb[:].rearrange("p (c q s) -> p c q s", c=DC, q=NQ, s=NS)
+
+        wg = []
+        for r, slots in enumerate((16, 8, 16, 16)):
+            wg_r = const.tile([P, slots * SLOT * 4], BF16, align_bytes=64, name="wg%d" % r)
+            wg.append(wg_r)
+        wgv = [w[:].bitcast(F32).rearrange("p (l c u) -> p l c u", c=SLOT, u=2) for w in wg]
+        nc.vector.memset(wgv[0][:, :, NQ:SLOT, :], 0.0)
+        nc.vector.memset(wgv[1][:, :, NQ:SLOT, :], 0.0)
+        nc.vector.memset(w1c[:, NS * SLOT :].bitcast(I32), 0)
+        nc.vector.memset(w1s[:, NS * SLOT :].bitcast(I32), 0)
+        nc.vector.memset(wgv[2][:, :, NS:SLOT, :], 0.0)
+        nc.vector.memset(wgv[3][:, :, NS:SLOT, :], 0.0)
+        nc.vector.memset(w2c[:, NQ * SLOT :].bitcast(I32), 0)
+        nc.vector.memset(w2s[:, NQ * SLOT :].bitcast(I32), 0)
+        nc.vector.memset(l2_sb[:], 0.0)
+
+        w32 = w_in[:].bitcast(F32)
+        for b in range(3):
+            wb = tpool.tile([P, 512], F32, tag="tb")
+            for cl in range(2):
+                for u in range(2):
+                    nc.tensor.transpose(
+                        wb[:, (2 * cl + u) * P : (2 * cl + u + 1) * P],
+                        w32[:, 2 * b + cl, u:256:2],
+                        ident[:],
+                    )
+            on_scalar = b != 1
+            wb_sq = wb[:].rearrange("p (c u s q) -> p c s q u", c=2, u=2, s=4, q=NQ)
+            wb_qs = wb[:].rearrange("p (c u s q) -> p c q s u", c=2, u=2, s=4, q=NQ)
+            for cl in range(2):
+                j = 2 * b + cl
+                s0 = 4 * j
+                copy_words(on_scalar, wgv[s0 // 16][:, s0 % 16 : s0 % 16 + 4, 0:NQ, :], wb_sq[:, cl])
+                for half in range(2):
+                    copy_words(
+                        on_scalar,
+                        wgv[2 + half][:, :, s0 : s0 + 4, :],
+                        wb_qs[:, cl, 16 * half : 16 * half + 16],
+                    )
+        nc.vector.quantize_mx(out=w1c[:, 0:1024].bitcast(FP8X4), scales=w1s[:, 0:1024], in_=wg[0][:])
+        nc.vector.quantize_mx(out=w1c[:, 1024:1536].bitcast(FP8X4), scales=w1s[:, 1024:1536], in_=wg[1][:])
+
+        t_banks = {}
+        grouped = {}
+        quant = {}
+        m_bank = {}
+        turned = {}
+
+        def piece_of(n, g):
+            start = 0
+            for pi, size in enumerate(PIECES[n]):
+                if g < start + size:
+                    return pi, g - start
+                start += size
+            return None
+
+        def transposes(k):
+            first, n = loads[k]
+            banks = []
+            for b in range((DC * n + 1) // 2):
+                tb = tpool.tile([P, 512], F32, tag="tb")
+                for cl in range(min(2, DC * n - 2 * b)):
+                    g = 2 * b + cl
+                    x32 = x_tiles[first + g // DC][:].bitcast(F32)
+                    dc = g % DC
+                    for h in range(2):
+                        nc.tensor.transpose(
+                            tb[:, (2 * cl + h) * P : (2 * cl + h + 1) * P],
+                            x32[:, dc * 256 + h : (dc + 1) * 256 : 2],
+                            ident[:],
+                        )
+                banks.append(tb)
+            t_banks[k] = banks
+            g_big = gpool.tile([P, 4096], BF16, align_bytes=64)
+            g_small = gpool.tile([P, 1024], BF16, align_bytes=64)
+            grouped[k] = (g_big, g_small)
+
+        def copy_bank(k, b):
+            n = loads[k][1]
+            chunks = min(2, DC * n - 2 * b)
+            pi, c0 = piece_of(n, 2 * b)
+            g32 = grouped[k][pi][:].bitcast(F32)
+            copy_words(
+                b not in VECTOR_BANKS[n],
+                g32[:, c0 * 256 : (c0 + chunks) * 256].rearrange("p (c d h) -> p c d h", c=chunks, d=P, h=2),
+                t_banks[k][b][:, 0 : chunks * 256].rearrange("p (c h d) -> p c d h", c=chunks, h=2, d=P),
+            )
+
+        def quantise(k):
+            sizes = PIECES[loads[k][1]]
+            c_big = qpool.tile([P, 1024], U32, align_bytes=64)
+            p_big = qpool.tile([P, 1024], U8, align_bytes=64)
+            c_small = qpool.tile([P, 256], U32, align_bytes=64)
+            p_small = qpool.tile([P, 256], U8, align_bytes=64)
+            quant[k] = ((c_big, p_big), (c_small, p_small))
+            for pi, size in enumerate(sizes):
+                codes, planes = quant[k][pi]
+                nc.vector.quantize_mx(
+                    out=codes[:, 0 : size * P].bitcast(FP8X4),
+                    scales=planes[:, 0 : size * P],
+                    in_=grouped[k][pi][:, 0 : size * 512],
+                )
+
+        def sum_squares(t):
+            for part, (c0, c1) in enumerate(((0, 4), (4, DC))):
+                dt_ps = tpool.tile([P, 512], F32, tag="tb")
+                for dc in range(c0, c1):
+                    nc.tensor.transpose(
+                        dt_ps[:, (dc - c0) * P : (dc - c0 + 1) * P], diffs[t % 3][:, dc * P : (dc + 1) * P], ident[:]
+                    )
+                turned[(t, part)] = dt_ps
+
+        def square_sums(t):
+            for part, width in enumerate((4 * P, P)):
+                junk = jpool.tile([P, 512], F32)
+                nc.scalar.activation(
+                    out=junk[:, 0:width],
+                    in_=turned[(t, part)][:, 0:width],
+                    func=ACT.Square,
+                    accum_out=acc[:, part, t : t + 1],
+                )
+
+        def mx_run(j):
+            x, d0, step, count, ready = runs[j]
+            is_q, t, h0, n, members = passes[x]
+            wc, ws = (w2c, w2s) if is_q else (w1c, w1s)
+            where = []
+            for k in members:
+                for il in range(loads[k][1]):
+                    where.append((k, il))
+            mb = mpool.tile([P, 512], F32, tag="m%d" % (j % 2))
+            for row in range(count):
+                dc = d0 + step * row
+                for i in range(n):
+                    k, il = where[i]
+                    pi, c0 = piece_of(loads[k][1], il * DC + dc)
+                    codes, planes = quant[k][pi]
+                    w0 = SLOT * (4 * t + h0 + i)
+                    col = BLK * (row * n + i)
+                    nc.tensor.matmul_mx(
+                        out=mb[:, col : col + P],
+                        lhsT=codes[:, c0 * P : (c0 + 1) * P].bitcast(FP8X4),
+                        lhsT_scale=planes[:, c0 * P : (c0 + 1) * P],
+                        rhs=wc[:, w0 : w0 + P].bitcast(FP8X4),
+                        rhs_scale=ws[:, w0 : w0 + P],
+                        start=True,
+                        stop=True,
+                    )
+            m_bank[j] = mb
+
+        def diff_view(j):
+            x, d0, step, count, ready = runs[j]
+            is_q, t, h0, n, members = passes[x]
+            dv = diffs[t % 3][:].rearrange("p (c i s) -> p c i s", c=DC, i=4, s=32)
+            return dv[:, d0 : d0 + step * (count - 1) + 1 : step, h0 : h0 + n, 0:NS]
+
+        def drain(j):
+            x, d0, step, count, ready = runs[j]
+            is_q, t, h0, n, members = passes[x]
+            first = 4 * t + h0
+            stop = d0 + step * (count - 1) + 1
+            used = m_bank[j][:, 0 : count * n * BLK]
+            if is_q:
+                nc.vector.tensor_tensor(
+                    out=diff_view(j),
+                    in0=cv[:, d0:stop:step, first : first + n, :],
+                    in1=used.rearrange("p (c i r) -> p c i r", c=count, i=n, r=BLK)[:, :, :, 0:NS],
+                    op=ALU.subtract,
+                )
+            else:
+                nc.vector.tensor_copy(
+                    out=cv[:, d0:stop:step, :, first : first + n],
+                    in_=used.rearrange("p (c i r) -> p c r i", c=count, i=n, r=BLK),
+                )
+
+        to_drain = []
+        next_run = 0
+        waiting = []
+        for k in range(n_loads + 8):
+            ending = k >= n_loads - 1
+            if ending and 0 <= k - 1 < n_loads:
+                quantise(k - 1)
+            drained = to_drain
+            to_drain = []
+            for j in drained:
+                drain(j)
+            complete = []
+            for j in drained:
+                x = runs[j][0]
+                is_q, t, h0, n4, members = passes[x]
+                if is_q and h0 + n4 == 4 and (j + 1 == len(runs) or runs[j + 1][0] != x):
+                    complete.append(t)
+            turn = [k] if k < n_loads - 2 else ([k, k + 1] if k == n_loads - 2 else [])
+            for kk in turn:
+                transposes(kk)
+                for il in range(loads[kk][1]):
+                    if len(x_tiles) < len(images):
+                        load_next()
+                        if len(x_tiles) == len(images):
+                            nc.sync.dma_start(out=sc_bf[:], in_=scale.partition_broadcast(P))
+            if not ending and 0 <= k - 1:
+                quantise(k - 1)
+            if k in W2_SLOTS:
+                half = W2_SLOTS.index(k)
+                nc.vector.quantize_mx(
+                    out=w2c[:, 1024 * half : 1024 * half + 1024].bitcast(FP8X4),
+                    scales=w2s[:, 1024 * half : 1024 * half + 1024],
+                    in_=wg[2 + half][:],
+                )
+            for kk in turn:
+                for b in range((DC * loads[kk][1] + 1) // 2):
+                    copy_bank(kk, b)
+            if k < n_loads:
+                for t in complete:
+                    sum_squares(t)
+                    square_sums(t)
+            if next_run < len(runs) and runs[next_run][4] <= k:
+                mx_run(next_run)
+                to_drain.append(next_run)
+                next_run += 1
+            if k >= n_loads:
+                waiting.extend(complete)
+                if next_run == len(runs):
+                    for t in waiting:
+                        sum_squares(t)
+                        square_sums(t)
+                    waiting = []
+
+        nc.vector.tensor_scalar(out=sc_f[:], in0=sc_bf[:], scalar1=LOGIT_FACTOR, scalar2=None, op0=ALU.mult)
+        nc.vector.tensor_tensor(out=l2_sb[:, 0:8], in0=acc[:, 0, :], in1=acc[:, 1, :], op=ALU.add)
+        fin = mpool.tile([P, 512], F32, tag="m0")
+        nc.tensor.transpose(fin[:, 0:P], l2_sb[:], ident[:])
+        z = const.tile([P, 4, NS], F32)
+        zs = const.tile([P, 4, NS], F32)
+        ez = const.tile([P, 4, NS], F32)
+        res = const.tile([P, 4, NS], F32)
+        mx = const.tile([P, 4], F32)
+        sm = const.tile([P, 4], F32)
+        ls = const.tile([P, 4], F32)
+        nc.vector.tensor_scalar(
+            out=z[:],
+            in0=fin[:, 0:P].rearrange("p (i s) -> p i s", i=4, s=32)[:, :, 0:NS],
+            scalar1=sc_f[:, 0:1],
+            scalar2=None,
+            op0=ALU.mult,
+        )
+        nc.vector.tensor_reduce(out=mx[:], in_=z[:], axis=AX.X, op=ALU.max)
+        nc.vector.tensor_tensor(out=zs[:], in0=z[:], in1=mx[:].unsqueeze(2).to_broadcast([P, 4, NS]), op=ALU.subtract)
+        nc.scalar.activation(out=ez[:], in_=zs[:], func=ACT.Exp)
+        nc.vector.tensor_reduce(out=sm[:], in_=ez[:], axis=AX.X, op=ALU.add)
+        nc.scalar.activation(out=ls[:], in_=sm[:], func=ACT.Ln)
+        nc.vector.tensor_tensor(out=res[:], in0=zs[:], in1=ls[:].unsqueeze(2).to_broadcast([P, 4, NS]), op=ALU.subtract)
+        nc.sync.dma_start(
+            out=out.rearrange("(t l) s -> t (l s)", l=4),
+            in_=res[0:8].rearrange("p l s -> p (l s)"),
+        )

@@ -19,14 +19,15 @@ P = 128
 NS = 24
 NQ = 32
 DC = 5
-X_BUFS = 14
+X_BUFS = 10
 SLOT = 64
 LAG = 2
 BLK = 32
 LOGIT_FACTOR = -1.0 / (600.0 * 512.0 * 512.0)
 
 PIECES = {2: (8, 2), 1: (4, 1)}
-VECTOR_BANKS = {2: (4,), 1: (2,)}
+VECTOR_BANKS = {2: (), 1: (2,)}
+PERM = 4
 FULL_QUAD = ((2, 2),)
 QUERY_QUADS = (FULL_QUAD,) * 7 + (((2,), (1, 1)),)
 W2_SLOTS = (2, 3)
@@ -63,6 +64,7 @@ def tile_proto_kernel(tc, feature_map, weight2, scale, out):
     with ExitStack() as ctx:
         const = ctx.enter_context(tc.tile_pool(name="const", bufs=1))
         xin = ctx.enter_context(tc.tile_pool(name="xin", bufs=X_BUFS))
+        ppool = ctx.enter_context(tc.tile_pool(name="ppool", bufs=3))
         gpool = ctx.enter_context(tc.tile_pool(name="gpool", bufs=4))
         qpool = ctx.enter_context(tc.tile_pool(name="qpool", bufs=5))
         tpool = ctx.enter_context(tc.psum_pool(name="tpool", bufs=6))
@@ -170,6 +172,22 @@ def tile_proto_kernel(tc, feature_map, weight2, scale, out):
                 start += size
             return None
 
+        permuted = {}
+
+        def permute(k):
+            first, n = loads[k]
+            if n != 2:
+                return
+            xp = ppool.tile([P, 2, PERM * 256], F32)
+            for il in range(n):
+                nc.vector.tensor_copy(
+                    out=xp[:, il, :].rearrange("p (c u w) -> p c u w", c=PERM, u=2, w=P),
+                    in_=x_tiles[first + il][:].bitcast(F32)[:, 0 : PERM * 256].rearrange(
+                        "p (c w u) -> p c u w", c=PERM, w=P, u=2
+                    ),
+                )
+            permuted[k] = xp
+
         def transposes(k):
             first, n = loads[k]
             banks = []
@@ -180,11 +198,11 @@ def tile_proto_kernel(tc, feature_map, weight2, scale, out):
                     x32 = x_tiles[first + g // DC][:].bitcast(F32)
                     dc = g % DC
                     for h in range(2):
-                        nc.tensor.transpose(
-                            tb[:, (2 * cl + h) * P : (2 * cl + h + 1) * P],
-                            x32[:, dc * 256 + h : (dc + 1) * 256 : 2],
-                            ident[:],
-                        )
+                        if k in permuted and dc < PERM:
+                            src = permuted[k][:, g // DC, dc * 256 + h * P : dc * 256 + (h + 1) * P]
+                        else:
+                            src = x32[:, dc * 256 + h : (dc + 1) * 256 : 2]
+                        nc.tensor.transpose(tb[:, (2 * cl + h) * P : (2 * cl + h + 1) * P], src, ident[:])
                 banks.append(tb)
             t_banks[k] = banks
             g_big = gpool.tile([P, 4096], BF16, align_bytes=64)
@@ -323,6 +341,8 @@ def tile_proto_kernel(tc, feature_map, weight2, scale, out):
                     scales=w2s[:, 1024 * half : 1024 * half + 1024],
                     in_=wg[2 + half][:],
                 )
+            if 0 < k + 1 < n_loads:
+                permute(k + 1)
             for kk in turn:
                 for b in range((DC * loads[kk][1] + 1) // 2):
                     copy_bank(kk, b)

@@ -19,66 +19,51 @@ P = 128
 NS = 24
 NQ = 32
 DC = 5
-X_BUFS = 10
-SLOT = 64
-LAG = 2
+X_BUFS = 6
 BLK = 32
+PAIR = 3 * BLK
 LOGIT_FACTOR = -1.0 / (600.0 * 512.0 * 512.0)
 
-PIECES = {2: (8, 2), 1: (4, 1)}
-VECTOR_BANKS = {2: (), 1: (2,)}
-PERM = 4
-FULL_QUAD = ((2, 2),)
-QUERY_QUADS = (FULL_QUAD,) * 7 + (((2,), (1, 1)),)
-W2_SLOTS = (2, 3)
+UNITS = 28
+PERM = 8
+FIRST_PERM = 1
+SDRAIN = (0, 1, 2, 3)
+SD_AT = 1
+VCOPY = {26: (3,), 27: (1, 3)}
+LAST_PERM = UNITS
+DIFF_BUFS = 3
 
 
 def tile_proto_kernel(tc, feature_map, weight2, scale, out):
     nc = tc.nc
-    loads = []
-    passes = []
-    images = []
-    for is_q, quads in ((False, (FULL_QUAD,) * (NS // 4)), (True, QUERY_QUADS)):
-        for t, quad in enumerate(quads):
-            h0 = 0
-            for group in quad:
-                members = []
-                for n in group:
-                    members.append(len(loads))
-                    loads.append((len(images), n))
-                    for il in range(n):
-                        images.append(4 * t + h0 + sum(loads[m][1] for m in members[:-1]) + il + (NS if is_q else 0))
-                total = sum(group)
-                passes.append((is_q, t, h0, total, members))
-                h0 += total
-    n_loads = len(loads)
-    runs = []
-    for x, entry in enumerate(passes):
-        ready = entry[4][-1] + LAG
-        if entry[3] == 4:
-            runs.append((x, 0, 2, 3, ready))
-            runs.append((x, 1, 2, 2, ready))
-        else:
-            runs.append((x, 0, 1, DC, ready))
-
     with ExitStack() as ctx:
         const = ctx.enter_context(tc.tile_pool(name="const", bufs=1))
         xin = ctx.enter_context(tc.tile_pool(name="xin", bufs=X_BUFS))
-        ppool = ctx.enter_context(tc.tile_pool(name="ppool", bufs=3))
-        gpool = ctx.enter_context(tc.tile_pool(name="gpool", bufs=4))
+        ppool = ctx.enter_context(tc.tile_pool(name="ppool", bufs=4))
+        gpool = ctx.enter_context(tc.tile_pool(name="gpool", bufs=3))
         qpool = ctx.enter_context(tc.tile_pool(name="qpool", bufs=5))
         tpool = ctx.enter_context(tc.psum_pool(name="tpool", bufs=6))
         mpool = ctx.enter_context(tc.psum_pool(name="mpool", bufs=1))
         jpool = ctx.enter_context(tc.tile_pool(name="jpool", bufs=2))
         ctx.enter_context(tc.manual_schedule())
 
-        x_tiles = []
+        x_tiles = {}
 
-        def load_next():
-            img = images[len(x_tiles)]
-            xt = xin.tile([P, DC * 512], BF16)
-            nc.sync.dma_start(out=xt[:], in_=feature_map[img].rearrange("(p c) m -> p (c m)", c=DC))
-            x_tiles.append(xt)
+        def load(k):
+            if k >= UNITS:
+                return
+            i0 = 2 * k
+            xt = xin.tile([P, 2, DC * 512], BF16)
+            if k in (0, UNITS - 1):
+                for il in range(2):
+                    nc.sync.dma_start(out=xt[:, il, :], in_=feature_map[i0 + il].rearrange("(p c) m -> p (c m)", c=DC))
+            else:
+                nc.sync.dma_start(
+                    out=xt[:], in_=feature_map[i0 : i0 + 2].rearrange("i (p c) m -> p i (c m)", c=DC)
+                )
+            if k == UNITS - 1:
+                nc.sync.dma_start(out=sc_bf[:], in_=scale.partition_broadcast(P))
+            x_tiles[k] = xt
 
         def copy_words(on_scalar, dst, src):
             if on_scalar:
@@ -93,43 +78,41 @@ def tile_proto_kernel(tc, feature_map, weight2, scale, out):
         )
         sc_bf = const.tile([P, 1], BF16)
         for k in range(X_BUFS):
-            load_next()
+            load(k)
 
         ident = const.tile([P, P], F32)
         make_identity(nc, ident[:])
         diffs = []
-        for r in range(3):
+        for r in range(DIFF_BUFS):
             dt_r = const.tile([P, DC * P], F32, name="diff%d" % r)
             nc.gpsimd.memset(dt_r[:], 0.0)
             diffs.append(dt_r)
 
         warm = const.tile([P, 1], F32)
-        nc.vector.memset(warm[:], 0.0)
+        nc.vector.memset(warm[:], 1.0)
         nc.scalar.activation(out=warm[:], in_=warm[:], func=ACT.Exp)
 
-        w1c = const.tile([P, (NS + 1) * SLOT], U32, align_bytes=64)
-        w1s = const.tile([P, (NS + 1) * SLOT], U8, align_bytes=64)
-        w2c = const.tile([P, (NQ + 1) * SLOT], U32, align_bytes=64)
-        w2s = const.tile([P, (NQ + 1) * SLOT], U8, align_bytes=64)
+        w1c = const.tile([P, (NS + 2) * BLK], U32, align_bytes=64)
+        w1s = const.tile([P, (NS + 2) * BLK], U8, align_bytes=64)
+        w2c = const.tile([P, (NQ + 2) * BLK], U32, align_bytes=64)
+        w2s = const.tile([P, (NQ + 2) * BLK], U8, align_bytes=64)
         c_sb = const.tile([P, DC * NQ * NS], F32)
         l2_sb = const.tile([P, P], F32)
         acc = const.tile([P, 2, 8], F32)
         sc_f = const.tile([P, 1], F32)
-        cv = c_sb[:].rearrange("p (c q s) -> p c q s", c=DC, q=NQ, s=NS)
+        cv = c_sb[:].rearrange("p (c s q) -> p c s q", c=DC, q=NQ, s=NS)
 
         wg = []
         for r, slots in enumerate((16, 8, 16, 16)):
-            wg_r = const.tile([P, slots * SLOT * 4], BF16, align_bytes=64, name="wg%d" % r)
+            wg_r = const.tile([P, slots * BLK * 4], BF16, align_bytes=64, name="wg%d" % r)
             wg.append(wg_r)
-        wgv = [w[:].bitcast(F32).rearrange("p (l c u) -> p l c u", c=SLOT, u=2) for w in wg]
-        nc.vector.memset(wgv[0][:, :, NQ:SLOT, :], 0.0)
-        nc.vector.memset(wgv[1][:, :, NQ:SLOT, :], 0.0)
-        nc.vector.memset(w1c[:, NS * SLOT :].bitcast(I32), 0)
-        nc.vector.memset(w1s[:, NS * SLOT :].bitcast(I32), 0)
-        nc.vector.memset(wgv[2][:, :, NS:SLOT, :], 0.0)
-        nc.vector.memset(wgv[3][:, :, NS:SLOT, :], 0.0)
-        nc.vector.memset(w2c[:, NQ * SLOT :].bitcast(I32), 0)
-        nc.vector.memset(w2s[:, NQ * SLOT :].bitcast(I32), 0)
+        wgv = [w[:].bitcast(F32).rearrange("p (l c u) -> p l c u", c=BLK, u=2) for w in wg]
+        nc.vector.memset(w1c[:, NS * BLK :].bitcast(I32), 0)
+        nc.vector.memset(w1s[:, NS * BLK :].bitcast(I32), 0)
+        nc.vector.memset(wgv[2][:, :, NS:BLK, :], 0.0)
+        nc.vector.memset(wgv[3][:, :, NS:BLK, :], 0.0)
+        nc.vector.memset(w2c[:, NQ * BLK :].bitcast(I32), 0)
+        nc.vector.memset(w2s[:, NQ * BLK :].bitcast(I32), 0)
         nc.vector.memset(l2_sb[:], 0.0)
 
         w32 = w_in[:].bitcast(F32)
@@ -155,233 +138,193 @@ def tile_proto_kernel(tc, feature_map, weight2, scale, out):
                         wgv[2 + half][:, :, s0 : s0 + 4, :],
                         wb_qs[:, cl, 16 * half : 16 * half + 16],
                     )
-        nc.vector.quantize_mx(out=w1c[:, 0:1024].bitcast(FP8X4), scales=w1s[:, 0:1024], in_=wg[0][:])
-        nc.vector.quantize_mx(out=w1c[:, 1024:1536].bitcast(FP8X4), scales=w1s[:, 1024:1536], in_=wg[1][:])
+        nc.vector.quantize_mx(out=w1c[:, 0:512].bitcast(FP8X4), scales=w1s[:, 0:512], in_=wg[0][:])
+        nc.vector.quantize_mx(out=w1c[:, 512:768].bitcast(FP8X4), scales=w1s[:, 512:768], in_=wg[1][:])
 
+        permuted = {}
         t_banks = {}
         grouped = {}
         quant = {}
-        m_bank = {}
         turned = {}
 
-        def piece_of(n, g):
-            start = 0
-            for pi, size in enumerate(PIECES[n]):
-                if g < start + size:
-                    return pi, g - start
-                start += size
-            return None
-
-        permuted = {}
-
         def permute(k):
-            first, n = loads[k]
-            if n != 2:
-                return
-            xp = ppool.tile([P, 2, PERM * 256], F32)
-            for il in range(n):
-                nc.vector.tensor_copy(
-                    out=xp[:, il, :].rearrange("p (c u w) -> p c u w", c=PERM, u=2, w=P),
-                    in_=x_tiles[first + il][:].bitcast(F32)[:, 0 : PERM * 256].rearrange(
-                        "p (c w u) -> p c u w", c=PERM, w=P, u=2
-                    ),
-                )
+            xp = ppool.tile([P, PERM * 256], F32)
+            nc.vector.tensor_copy(
+                out=xp[:].rearrange("p (g u w) -> p g u w", g=PERM, u=2, w=P),
+                in_=x_tiles[k][:].rearrange("p i m -> p (i m)").bitcast(F32)[:, 0 : PERM * 256].rearrange(
+                    "p (g w u) -> p g u w", g=PERM, w=P, u=2
+                ),
+            )
             permuted[k] = xp
 
         def transposes(k):
-            first, n = loads[k]
+            x32 = x_tiles[k][:].rearrange("p i m -> p (i m)").bitcast(F32)
             banks = []
-            for b in range((DC * n + 1) // 2):
+            for b in range(DC):
                 tb = tpool.tile([P, 512], F32, tag="tb")
-                for cl in range(min(2, DC * n - 2 * b)):
-                    g = 2 * b + cl
-                    x32 = x_tiles[first + g // DC][:].bitcast(F32)
-                    dc = g % DC
+                for g in (2 * b, 2 * b + 1):
                     for h in range(2):
-                        if k in permuted and dc < PERM:
-                            src = permuted[k][:, g // DC, dc * 256 + h * P : dc * 256 + (h + 1) * P]
+                        if k in permuted and g < PERM:
+                            src = permuted[k][:, g * 256 + h * P : g * 256 + (h + 1) * P]
                         else:
-                            src = x32[:, dc * 256 + h : (dc + 1) * 256 : 2]
-                        nc.tensor.transpose(tb[:, (2 * cl + h) * P : (2 * cl + h + 1) * P], src, ident[:])
+                            src = x32[:, g * 256 + h : (g + 1) * 256 : 2]
+                        at = (2 * (g - 2 * b) + h) * P
+                        nc.tensor.transpose(tb[:, at : at + P], src, ident[:])
                 banks.append(tb)
             t_banks[k] = banks
-            g_big = gpool.tile([P, 4096], BF16, align_bytes=64)
-            g_small = gpool.tile([P, 1024], BF16, align_bytes=64)
-            grouped[k] = (g_big, g_small)
+            g_tile = gpool.tile([P, 2 * DC * 512], BF16, align_bytes=64)
+            grouped[k] = g_tile
+            c_tile = qpool.tile([P, 2 * DC * P], U32, align_bytes=64)
+            s_tile = qpool.tile([P, 2 * DC * P], U8, align_bytes=64)
+            quant[k] = (c_tile, s_tile)
 
-        def copy_bank(k, b):
-            n = loads[k][1]
-            chunks = min(2, DC * n - 2 * b)
-            pi, c0 = piece_of(n, 2 * b)
-            g32 = grouped[k][pi][:].bitcast(F32)
+        def copy_bank(k, b, on_scalar):
             copy_words(
-                b not in VECTOR_BANKS[n],
-                g32[:, c0 * 256 : (c0 + chunks) * 256].rearrange("p (c d h) -> p c d h", c=chunks, d=P, h=2),
-                t_banks[k][b][:, 0 : chunks * 256].rearrange("p (c h d) -> p c d h", c=chunks, h=2, d=P),
+                on_scalar,
+                grouped[k][:].bitcast(F32)[:, b * 512 : (b + 1) * 512].rearrange("p (c d h) -> p c d h", c=2, d=P, h=2),
+                t_banks[k][b][:].rearrange("p (c h d) -> p c d h", c=2, h=2, d=P),
             )
 
-        def quantise(k):
-            sizes = PIECES[loads[k][1]]
-            c_big = qpool.tile([P, 1024], U32, align_bytes=64)
-            p_big = qpool.tile([P, 1024], U8, align_bytes=64)
-            c_small = qpool.tile([P, 256], U32, align_bytes=64)
-            p_small = qpool.tile([P, 256], U8, align_bytes=64)
-            quant[k] = ((c_big, p_big), (c_small, p_small))
-            for pi, size in enumerate(sizes):
-                codes, planes = quant[k][pi]
-                nc.vector.quantize_mx(
-                    out=codes[:, 0 : size * P].bitcast(FP8X4),
-                    scales=planes[:, 0 : size * P],
-                    in_=grouped[k][pi][:, 0 : size * 512],
-                )
+        def quantise(k, g0, g1):
+            codes, planes = quant[k]
+            nc.vector.quantize_mx(
+                out=codes[:, g0 * P : g1 * P].bitcast(FP8X4),
+                scales=planes[:, g0 * P : g1 * P],
+                in_=grouped[k][:, g0 * 512 : g1 * 512],
+            )
 
-        def sum_squares(t):
-            for part, (c0, c1) in enumerate(((0, 4), (4, DC))):
-                dt_ps = tpool.tile([P, 512], F32, tag="tb")
-                for dc in range(c0, c1):
-                    nc.tensor.transpose(
-                        dt_ps[:, (dc - c0) * P : (dc - c0 + 1) * P], diffs[t % 3][:, dc * P : (dc + 1) * P], ident[:]
-                    )
-                turned[(t, part)] = dt_ps
-
-        def square_sums(t):
-            for part, width in enumerate((4 * P, P)):
-                junk = jpool.tile([P, 512], F32)
-                nc.scalar.activation(
-                    out=junk[:, 0:width],
-                    in_=turned[(t, part)][:, 0:width],
-                    func=ACT.Square,
-                    accum_out=acc[:, part, t : t + 1],
-                )
-
-        def mx_run(j):
-            x, d0, step, count, ready = runs[j]
-            is_q, t, h0, n, members = passes[x]
-            wc, ws = (w2c, w2s) if is_q else (w1c, w1s)
-            where = []
-            for k in members:
-                for il in range(loads[k][1]):
-                    where.append((k, il))
-            mb = mpool.tile([P, 512], F32, tag="m%d" % (j % 2))
-            for row in range(count):
-                dc = d0 + step * row
-                for i in range(n):
-                    k, il = where[i]
-                    pi, c0 = piece_of(loads[k][1], il * DC + dc)
-                    codes, planes = quant[k][pi]
-                    w0 = SLOT * (4 * t + h0 + i)
-                    col = BLK * (row * n + i)
+        def mx_run(k, d0, d1, pool, tag):
+            codes, planes = quant[k]
+            wc, ws, w0 = (w2c, w2s, BLK * (2 * k - NS)) if 2 * k >= NS else (w1c, w1s, BLK * 2 * k)
+            mb = pool.tile([P, 512], F32, tag=tag)
+            for row in range(d1 - d0):
+                for il in range(2):
+                    g = il * DC + d0 + row
+                    col = PAIR * row + BLK * il
+                    width = P if col + P <= 512 else 2 * BLK
                     nc.tensor.matmul_mx(
-                        out=mb[:, col : col + P],
-                        lhsT=codes[:, c0 * P : (c0 + 1) * P].bitcast(FP8X4),
-                        lhsT_scale=planes[:, c0 * P : (c0 + 1) * P],
-                        rhs=wc[:, w0 : w0 + P].bitcast(FP8X4),
-                        rhs_scale=ws[:, w0 : w0 + P],
+                        out=mb[:, col : col + width],
+                        lhsT=codes[:, g * P : (g + 1) * P].bitcast(FP8X4),
+                        lhsT_scale=planes[:, g * P : (g + 1) * P],
+                        rhs=wc[:, w0 : w0 + width].bitcast(FP8X4),
+                        rhs_scale=ws[:, w0 : w0 + width],
                         start=True,
                         stop=True,
                     )
-            m_bank[j] = mb
+            return (k, d0, d1, mb)
 
-        def diff_view(j):
-            x, d0, step, count, ready = runs[j]
-            is_q, t, h0, n, members = passes[x]
-            dv = diffs[t % 3][:].rearrange("p (c i s) -> p c i s", c=DC, i=4, s=32)
-            return dv[:, d0 : d0 + step * (count - 1) + 1 : step, h0 : h0 + n, 0:NS]
-
-        def drain(j):
-            x, d0, step, count, ready = runs[j]
-            is_q, t, h0, n, members = passes[x]
-            first = 4 * t + h0
-            stop = d0 + step * (count - 1) + 1
-            used = m_bank[j][:, 0 : count * n * BLK]
-            if is_q:
+        def drain(run):
+            k, d0, d1, mb = run
+            used = mb[:, 0 : (d1 - d0) * PAIR].rearrange("p (c j r) -> p c j r", j=3, r=BLK)[:, :, 0:3:2, :]
+            if 2 * k >= NS:
+                i0 = 2 * k - NS
+                dv = diffs[i0 // 4 % DIFF_BUFS][:].rearrange("p (c i s) -> p c i s", c=DC, i=4, s=32)
                 nc.vector.tensor_tensor(
-                    out=diff_view(j),
-                    in0=cv[:, d0:stop:step, first : first + n, :],
-                    in1=used.rearrange("p (c i r) -> p c i r", c=count, i=n, r=BLK)[:, :, :, 0:NS],
+                    out=dv[:, d0:d1, i0 % 4 : i0 % 4 + 2, 0:NS],
+                    in0=cv[:, d0:d1, :, i0 : i0 + 2].rearrange("p c s i -> p c i s"),
+                    in1=used[:, :, :, 0:NS],
                     op=ALU.subtract,
                 )
             else:
-                nc.vector.tensor_copy(
-                    out=cv[:, d0:stop:step, :, first : first + n],
-                    in_=used.rearrange("p (c i r) -> p c r i", c=count, i=n, r=BLK),
+                copy_words(
+                    k in SDRAIN,
+                    cv[:, d0:d1, 2 * k : 2 * k + 2, :],
+                    used,
                 )
 
-        to_drain = []
-        next_run = 0
-        waiting = []
-        for k in range(n_loads + 8):
-            ending = k >= n_loads - 1
-            if ending and 0 <= k - 1 < n_loads:
-                quantise(k - 1)
-            drained = to_drain
-            to_drain = []
-            for j in drained:
-                drain(j)
-            complete = []
-            for j in drained:
-                x = runs[j][0]
-                is_q, t, h0, n4, members = passes[x]
-                if is_q and h0 + n4 == 4 and (j + 1 == len(runs) or runs[j + 1][0] != x):
-                    complete.append(t)
-            turn = [k] if k < n_loads - 2 else ([k, k + 1] if k == n_loads - 2 else [])
-            for kk in turn:
-                transposes(kk)
-                for il in range(loads[kk][1]):
-                    if len(x_tiles) < len(images):
-                        load_next()
-                        if len(x_tiles) == len(images):
-                            nc.sync.dma_start(out=sc_bf[:], in_=scale.partition_broadcast(P))
-            if not ending and 0 <= k - 1:
-                quantise(k - 1)
-            if k in W2_SLOTS:
-                half = W2_SLOTS.index(k)
+        def turn_diffs(t, part, c0, c1):
+            dt_ps = tpool.tile([P, 512], F32, tag="tb")
+            for dc in range(c0, c1):
+                nc.tensor.transpose(
+                    dt_ps[:, (dc - c0) * P : (dc - c0 + 1) * P],
+                    diffs[t % DIFF_BUFS][:, dc * P : (dc + 1) * P],
+                    ident[:],
+                )
+            turned[(t, part)] = (dt_ps, (c1 - c0) * P)
+
+        def square_sum(t, part):
+            dt_ps, width = turned[(t, part)]
+            junk = jpool.tile([P, 512], F32)
+            nc.scalar.activation(
+                out=junk[:, 0:width],
+                in_=dt_ps[:, 0:width],
+                func=ACT.Square,
+                accum_out=acc[:, part, t : t + 1],
+            )
+
+        def turn_and_square(t):
+            for part, (c0, c1) in enumerate(((0, 3), (3, DC))):
+                turn_diffs(t, part, c0, c1)
+                square_sum(t, part)
+
+        runs = []
+        to_turn = []
+        for k in range(UNITS):
+            if k == UNITS - 1:
+                quantise(k - 1, 0, 4)
+                quantise(k - 1, 4, 8)
+                quantise(k - 1, 8, 10)
+            elif k >= 1:
+                quantise(k - 1, 0, 8)
+                quantise(k - 1, 8, 10)
+            turn_now = to_turn
+            to_turn = []
+            late = [run for run in runs if run[0] in SDRAIN]
+            for run in runs:
+                if run[0] not in SDRAIN:
+                    drain(run)
+                if 2 * run[0] >= NS and run[0] % 2 == 1:
+                    to_turn.append((2 * run[0] - NS) // 4)
+            runs = []
+            for kk in ((FIRST_PERM, FIRST_PERM + 1) if k == FIRST_PERM - 2 + 1 else (k + 2,)):
+                if FIRST_PERM <= kk < LAST_PERM and kk not in permuted:
+                    permute(kk)
+            transposes(k)
+            load(k + X_BUFS)
+            if 2 <= k < 6:
+                half, part = (k - 2) // 2, (k - 2) % 2
+                col = 512 * half + 256 * part
                 nc.vector.quantize_mx(
-                    out=w2c[:, 1024 * half : 1024 * half + 1024].bitcast(FP8X4),
-                    scales=w2s[:, 1024 * half : 1024 * half + 1024],
-                    in_=wg[2 + half][:],
+                    out=w2c[:, col : col + 256].bitcast(FP8X4),
+                    scales=w2s[:, col : col + 256],
+                    in_=wg[2 + half][:, 1024 * part : 1024 * (part + 1)],
                 )
-            if 0 < k + 1 < n_loads:
-                permute(k + 1)
-            for kk in turn:
-                for b in range((DC * loads[kk][1] + 1) // 2):
-                    copy_bank(kk, b)
-            if k < n_loads:
-                for t in complete:
-                    sum_squares(t)
-                    square_sums(t)
-            if next_run < len(runs) and runs[next_run][4] <= k:
-                mx_run(next_run)
-                to_drain.append(next_run)
-                next_run += 1
-            if k >= n_loads:
-                waiting.extend(complete)
-                if next_run == len(runs):
-                    for t in waiting:
-                        sum_squares(t)
-                        square_sums(t)
-                    waiting = []
+            for b in range(DC):
+                copy_bank(k, b, b not in VCOPY.get(k, ()))
+                if b == SD_AT:
+                    for run in late:
+                        drain(run)
+            for t in turn_now:
+                turn_and_square(t)
+            if k % 2 == 1 and k >= 3:
+                runs = [mx_run(k - 3, 0, DC, mpool, "m0"), mx_run(k - 2, 0, DC, mpool, "m1")]
 
+        for g0, g1 in ((0, 4), (4, 8), (8, 10)):
+            quantise(27, g0, g1)
+        runs.append(mx_run(26, 0, DC, tpool, "tb"))
+        runs.append(mx_run(27, 0, 3, tpool, "tb"))
+        runs.append(mx_run(27, 3, DC, tpool, "tb"))
+        for run in runs:
+            drain(run)
+        turn_and_square(6)
+        turn_and_square(7)
         nc.vector.tensor_scalar(out=sc_f[:], in0=sc_bf[:], scalar1=LOGIT_FACTOR, scalar2=None, op0=ALU.mult)
-        nc.vector.tensor_tensor(out=l2_sb[:, 0:8], in0=acc[:, 0, :], in1=acc[:, 1, :], op=ALU.add)
-        fin = mpool.tile([P, 512], F32, tag="m0")
+        part = const.tile([P, 8], F32)
+        nc.vector.tensor_scalar(out=part[:], in0=acc[:, 0, :], scalar1=sc_f[:, 0:1], scalar2=None, op0=ALU.mult)
+        nc.vector.scalar_tensor_tensor(
+            out=l2_sb[:, 0:8], in0=acc[:, 1, :], scalar=sc_f[:, 0:1], in1=part[:], op0=ALU.mult, op1=ALU.add
+        )
+        fin = mpool.tile([P, 512], F32, tag="m1")
         nc.tensor.transpose(fin[:, 0:P], l2_sb[:], ident[:])
-        z = const.tile([P, 4, NS], F32)
+        z = fin[:, 0:P].rearrange("p (i s) -> p i s", i=4, s=32)[:, :, 0:NS]
         zs = const.tile([P, 4, NS], F32)
         ez = const.tile([P, 4, NS], F32)
         res = const.tile([P, 4, NS], F32)
         mx = const.tile([P, 4], F32)
         sm = const.tile([P, 4], F32)
         ls = const.tile([P, 4], F32)
-        nc.vector.tensor_scalar(
-            out=z[:],
-            in0=fin[:, 0:P].rearrange("p (i s) -> p i s", i=4, s=32)[:, :, 0:NS],
-            scalar1=sc_f[:, 0:1],
-            scalar2=None,
-            op0=ALU.mult,
-        )
-        nc.vector.tensor_reduce(out=mx[:], in_=z[:], axis=AX.X, op=ALU.max)
-        nc.vector.tensor_tensor(out=zs[:], in0=z[:], in1=mx[:].unsqueeze(2).to_broadcast([P, 4, NS]), op=ALU.subtract)
+        nc.vector.tensor_reduce(out=mx[:], in_=z, axis=AX.X, op=ALU.max)
+        nc.vector.tensor_tensor(out=zs[:], in0=z, in1=mx[:].unsqueeze(2).to_broadcast([P, 4, NS]), op=ALU.subtract)
         nc.scalar.activation(out=ez[:], in_=zs[:], func=ACT.Exp)
         nc.vector.tensor_reduce(out=sm[:], in_=ez[:], axis=AX.X, op=ALU.add)
         nc.scalar.activation(out=ls[:], in_=sm[:], func=ACT.Ln)

@@ -100,7 +100,7 @@ def tile_proto_kernel(tc, feature_map, weight2, scale, out):
         l2_sb = const.tile([P, P], F32)
         acc = const.tile([P, 2, 8], F32)
         sc_f = const.tile([P, 1], F32)
-        cv = c_sb[:].rearrange("p (c s q) -> p c s q", c=DC, q=NQ, s=NS)
+        cv = c_sb[:].rearrange("p (c k q i) -> p c k q i", c=DC, k=NS // 2, q=NQ, i=2)
 
         wg = []
         for r, slots in enumerate((16, 8, 16, 16)):
@@ -219,17 +219,18 @@ def tile_proto_kernel(tc, feature_map, weight2, scale, out):
             if 2 * k >= NS:
                 i0 = 2 * k - NS
                 dv = diffs[i0 // 4 % DIFF_BUFS][:].rearrange("p (c i s) -> p c i s", c=DC, i=4, s=32)
-                nc.vector.tensor_tensor(
-                    out=dv[:, d0:d1, i0 % 4 : i0 % 4 + 2, 0:NS],
-                    in0=cv[:, d0:d1, :, i0 : i0 + 2].rearrange("p c s i -> p c i s"),
-                    in1=used[:, :, :, 0:NS],
-                    op=ALU.subtract,
-                )
+                for il in range(2):
+                    nc.vector.tensor_tensor(
+                        out=dv[:, d0:d1, i0 % 4 + il, 0:NS].rearrange("p c (k i) -> p c k i", i=2),
+                        in0=cv[:, d0:d1, :, i0 + il, :],
+                        in1=used[:, :, il, 0:NS].rearrange("p c (k i) -> p c k i", i=2),
+                        op=ALU.subtract,
+                    )
             else:
                 copy_words(
                     k in SDRAIN,
-                    cv[:, d0:d1, 2 * k : 2 * k + 2, :],
-                    used,
+                    cv[:, d0:d1, k, :, :],
+                    used.rearrange("p c i r -> p c r i"),
                 )
 
         def turn_diffs(t, part, c0, c1):
@@ -296,8 +297,8 @@ def tile_proto_kernel(tc, feature_map, weight2, scale, out):
                         drain(run)
             for t in turn_now:
                 turn_and_square(t)
-            if k % 2 == 1 and k >= 3:
-                runs = [mx_run(k - 3, 0, DC, mpool, "m0"), mx_run(k - 2, 0, DC, mpool, "m1")]
+            if k >= 2:
+                runs = [mx_run(k - 2, 0, DC, mpool, "m%d" % (k % 2))]
 
         for g0, g1 in ((0, 4), (4, 8), (8, 10)):
             quantise(27, g0, g1)

@@ -25,12 +25,9 @@ PAIR = 3 * BLK
 LOGIT_FACTOR = -1.0 / (600.0 * 512.0 * 512.0)
 
 UNITS = 28
-PERM = 8
-FIRST_PERM = 1
 SDRAIN = (0, 1, 2, 3)
 SD_AT = 1
 VCOPY = {26: (3,), 27: (1, 3)}
-LAST_PERM = UNITS
 DIFF_BUFS = 3
 
 
@@ -76,6 +73,7 @@ def tile_proto_kernel(tc, feature_map, weight2, scale, out):
             out=w_in[:],
             in_=weight2.rearrange("s q m -> (s q) m").rearrange("(j p) m -> p j m", p=P),
         )
+        w_first = const.tile([P, 6 * P], F32)
         sc_bf = const.tile([P, 1], BF16)
         for k in range(X_BUFS):
             load(k)
@@ -115,59 +113,46 @@ def tile_proto_kernel(tc, feature_map, weight2, scale, out):
         nc.vector.memset(w2s[:, NQ * BLK :].bitcast(I32), 0)
         nc.vector.memset(l2_sb[:], 0.0)
 
-        w32 = w_in[:].bitcast(F32)
-        for b in range(3):
-            wb = tpool.tile([P, 512], F32, tag="tb")
-            for cl in range(2):
-                for u in range(2):
-                    nc.tensor.transpose(
-                        wb[:, (2 * cl + u) * P : (2 * cl + u + 1) * P],
-                        w32[:, 2 * b + cl, u:256:2],
-                        ident[:],
-                    )
-            on_scalar = b != 1
-            wb_sq = wb[:].rearrange("p (c u s q) -> p c s q u", c=2, u=2, s=4, q=NQ)
-            wb_qs = wb[:].rearrange("p (c u s q) -> p c q s u", c=2, u=2, s=4, q=NQ)
-            for cl in range(2):
-                j = 2 * b + cl
-                s0 = 4 * j
-                copy_words(on_scalar, wgv[s0 // 16][:, s0 % 16 : s0 % 16 + 4, 0:NQ, :], wb_sq[:, cl])
-                for half in range(2):
-                    copy_words(
-                        on_scalar,
-                        wgv[2 + half][:, :, s0 : s0 + 4, :],
-                        wb_qs[:, cl, 16 * half : 16 * half + 16],
-                    )
-        nc.vector.quantize_mx(out=w1c[:, 0:512].bitcast(FP8X4), scales=w1s[:, 0:512], in_=wg[0][:])
-        nc.vector.quantize_mx(out=w1c[:, 512:768].bitcast(FP8X4), scales=w1s[:, 512:768], in_=wg[1][:])
-
         permuted = {}
         t_banks = {}
         grouped = {}
         quant = {}
         turned = {}
 
-        def permute(k):
-            xp = ppool.tile([P, PERM * 256], F32)
+        def halves(words, chunks):
+            return words.rearrange("p (c s j v e) -> p c s j v e", c=chunks, s=2, j=8, v=2, e=8)
+
+        def gather(first, words, chunks, s):
             nc.vector.tensor_copy(
-                out=xp[:].rearrange("p (g u w) -> p g u w", g=PERM, u=2, w=P),
-                in_=x_tiles[k][:].rearrange("p i m -> p (i m)").bitcast(F32)[:, 0 : PERM * 256].rearrange(
-                    "p (g w u) -> p g u w", g=PERM, w=P, u=2
-                ),
+                out=first.rearrange("p (c j s e) -> p c s j e", c=chunks, s=2, j=8, e=8)[:, :, s],
+                in_=halves(words, chunks)[:, :, s, :, 0, :],
             )
-            permuted[k] = xp
+
+        def fill(words, chunks):
+            h = halves(words, chunks)
+            nc.vector.tensor_copy(out=h[:, :, 1, :, 0, :], in_=h[:, :, 0, :, 1, :])
+
+        def x_words(k):
+            return x_tiles[k][:].rearrange("p i m -> p (i m)").bitcast(F32)
+
+        def regroup(k, part, c0=0, c1=2 * DC):
+            if k not in permuted:
+                xp = ppool.tile([P, 2 * DC * P], F32)
+                permuted[k] = xp
+            words = x_words(k)[:, c0 * 256 : c1 * 256]
+            if part < 2:
+                gather(permuted[k][:, c0 * P : c1 * P], words, c1 - c0, part)
+            else:
+                fill(words, c1 - c0)
 
         def transposes(k):
-            x32 = x_tiles[k][:].rearrange("p i m -> p (i m)").bitcast(F32)
+            x32 = x_words(k)
             banks = []
             for b in range(DC):
                 tb = tpool.tile([P, 512], F32, tag="tb")
                 for g in (2 * b, 2 * b + 1):
                     for h in range(2):
-                        if k in permuted and g < PERM:
-                            src = permuted[k][:, g * 256 + h * P : g * 256 + (h + 1) * P]
-                        else:
-                            src = x32[:, g * 256 + h : (g + 1) * 256 : 2]
+                        src = x32[:, g * 256 + P : (g + 1) * 256] if h else permuted[k][:, g * P : (g + 1) * P]
                         at = (2 * (g - 2 * b) + h) * P
                         nc.tensor.transpose(tb[:, at : at + P], src, ident[:])
                 banks.append(tb)
@@ -258,16 +243,52 @@ def tile_proto_kernel(tc, feature_map, weight2, scale, out):
                 turn_diffs(t, part, c0, c1)
                 square_sum(t, part)
 
+        w32 = w_in[:].rearrange("p j m -> p (j m)").bitcast(F32)
+        for s in range(2):
+            gather(w_first[:], w32, 6, s)
+        fill(w32, 6)
+        for b in range(3):
+            wb = tpool.tile([P, 512], F32, tag="tb")
+            for cl in range(2):
+                for u in range(2):
+                    nc.tensor.transpose(
+                        wb[:, (2 * cl + u) * P : (2 * cl + u + 1) * P],
+                        w32[:, (2 * b + cl) * 256 + P : (2 * b + cl + 1) * 256]
+                        if u
+                        else w_first[:, (2 * b + cl) * P : (2 * b + cl + 1) * P],
+                        ident[:],
+                    )
+            on_scalar = b != 1
+            wb_sq = wb[:].rearrange("p (c u s q) -> p c s q u", c=2, u=2, s=4, q=NQ)
+            wb_qs = wb[:].rearrange("p (c u s q) -> p c q s u", c=2, u=2, s=4, q=NQ)
+            for cl in range(2):
+                j = 2 * b + cl
+                s0 = 4 * j
+                copy_words(on_scalar, wgv[s0 // 16][:, s0 % 16 : s0 % 16 + 4, 0:NQ, :], wb_sq[:, cl])
+                for half in range(2):
+                    copy_words(
+                        on_scalar,
+                        wgv[2 + half][:, :, s0 : s0 + 4, :],
+                        wb_qs[:, cl, 16 * half : 16 * half + 16],
+                    )
+        nc.vector.quantize_mx(out=w1c[:, 0:512].bitcast(FP8X4), scales=w1s[:, 0:512], in_=wg[0][:])
+        nc.vector.quantize_mx(out=w1c[:, 512:768].bitcast(FP8X4), scales=w1s[:, 512:768], in_=wg[1][:])
+
+        for k in range(2):
+            for c0, c1 in ((0, DC), (DC, 2 * DC)) if k == 0 else ((0, 2 * DC),):
+                for part in range(3):
+                    regroup(k, part, c0, c1)
         runs = []
         to_turn = []
         for k in range(UNITS):
+            ahead = 2 <= k + 2 < UNITS
             if k == UNITS - 1:
                 quantise(k - 1, 0, 4)
                 quantise(k - 1, 4, 8)
-                quantise(k - 1, 8, 10)
             elif k >= 1:
                 quantise(k - 1, 0, 8)
-                quantise(k - 1, 8, 10)
+            if ahead:
+                regroup(k + 2, 0)
             turn_now = to_turn
             to_turn = []
             late = [run for run in runs if run[0] in SDRAIN]
@@ -277,9 +298,12 @@ def tile_proto_kernel(tc, feature_map, weight2, scale, out):
                 if 2 * run[0] >= NS and run[0] % 2 == 1:
                     to_turn.append((2 * run[0] - NS) // 4)
             runs = []
-            for kk in ((FIRST_PERM, FIRST_PERM + 1) if k == FIRST_PERM - 2 + 1 else (k + 2,)):
-                if FIRST_PERM <= kk < LAST_PERM and kk not in permuted:
-                    permute(kk)
+            if ahead:
+                regroup(k + 2, 1)
+            if k >= 1:
+                quantise(k - 1, 8, 10)
+            if ahead:
+                regroup(k + 2, 2)
             transposes(k)
             load(k + X_BUFS)
             if 2 <= k < 6:

@@ -122,10 +122,10 @@ def tile_proto_kernel(tc, feature_map, weight2, scale, out):
         def halves(words, chunks):
             return words.rearrange("p (c s j v e) -> p c s j v e", c=chunks, s=2, j=8, v=2, e=8)
 
-        def gather(first, words, chunks, s):
+        def gather(first, words, chunks):
             nc.vector.tensor_copy(
-                out=first.rearrange("p (c j s e) -> p c s j e", c=chunks, s=2, j=8, e=8)[:, :, s],
-                in_=halves(words, chunks)[:, :, s, :, 0, :],
+                out=first.rearrange("p (c j s e) -> p c s j e", c=chunks, s=2, j=8, e=8),
+                in_=halves(words, chunks)[:, :, :, :, 0, :],
             )
 
         def fill(words, chunks):
@@ -140,8 +140,8 @@ def tile_proto_kernel(tc, feature_map, weight2, scale, out):
                 xp = ppool.tile([P, 2 * DC * P], F32)
                 permuted[k] = xp
             words = x_words(k)[:, c0 * 256 : c1 * 256]
-            if part < 2:
-                gather(permuted[k][:, c0 * P : c1 * P], words, c1 - c0, part)
+            if part == 0:
+                gather(permuted[k][:, c0 * P : c1 * P], words, c1 - c0)
             else:
                 fill(words, c1 - c0)
 
@@ -244,9 +244,10 @@ def tile_proto_kernel(tc, feature_map, weight2, scale, out):
                 square_sum(t, part)
 
         w32 = w_in[:].rearrange("p j m -> p (j m)").bitcast(F32)
-        for s in range(2):
-            gather(w_first[:], w32, 6, s)
+        gather(w_first[:], w32, 6)
         fill(w32, 6)
+        for part in range(2):
+            regroup(0, part, 0, DC)
         for b in range(3):
             wb = tpool.tile([P, 512], F32, tag="tb")
             for cl in range(2):
@@ -271,13 +272,13 @@ def tile_proto_kernel(tc, feature_map, weight2, scale, out):
                         wgv[2 + half][:, :, s0 : s0 + 4, :],
                         wb_qs[:, cl, 16 * half : 16 * half + 16],
                     )
+        for part in range(2):
+            regroup(0, part, DC, 2 * DC)
         nc.vector.quantize_mx(out=w1c[:, 0:512].bitcast(FP8X4), scales=w1s[:, 0:512], in_=wg[0][:])
         nc.vector.quantize_mx(out=w1c[:, 512:768].bitcast(FP8X4), scales=w1s[:, 512:768], in_=wg[1][:])
 
-        for k in range(2):
-            for c0, c1 in ((0, DC), (DC, 2 * DC)) if k == 0 else ((0, 2 * DC),):
-                for part in range(3):
-                    regroup(k, part, c0, c1)
+        for part in range(2):
+            regroup(1, part)
         runs = []
         to_turn = []
         for k in range(UNITS):
@@ -298,12 +299,10 @@ def tile_proto_kernel(tc, feature_map, weight2, scale, out):
                 if 2 * run[0] >= NS and run[0] % 2 == 1:
                     to_turn.append((2 * run[0] - NS) // 4)
             runs = []
-            if ahead:
-                regroup(k + 2, 1)
             if k >= 1:
                 quantise(k - 1, 8, 10)
             if ahead:
-                regroup(k + 2, 2)
+                regroup(k + 2, 1)
             transposes(k)
             load(k + X_BUFS)
             if 2 <= k < 6:

from contextlib import ExitStack

import concourse.mybir as mybir
from concourse.masks import make_identity

FLOPS = 2 * 2 * 24 * 32 * 640 * 512

F32 = mybir.dt.float32
BF16 = mybir.dt.bfloat16
U32 = mybir.dt.uint32
U8 = mybir.dt.uint8
I32 = mybir.dt.int32
FP8X4 = mybir.dt.float8_e4m3fn_x4
ALU = mybir.AluOpType
ACT = mybir.ActivationFunctionType
AX = mybir.AxisListType

P = 128
NS = 24
NQ = 32
DC = 5
X_BUFS = 6
BLK = 32
PAIR = 3 * BLK
LOGIT_FACTOR = -1.0 / (600.0 * 512.0 * 512.0)

UNITS = 28
SDRAIN = (0, 1, 2, 3)
SD_AT = 1
VCOPY = {26: (3,), 27: (1, 3)}
DIFF_BUFS = 3


def tile_proto_kernel(tc, feature_map, weight2, scale, out):
    nc = tc.nc
    with ExitStack() as ctx:
        const = ctx.enter_context(tc.tile_pool(name="const", bufs=1))
        xin = ctx.enter_context(tc.tile_pool(name="xin", bufs=X_BUFS))
        ppool = ctx.enter_context(tc.tile_pool(name="ppool", bufs=4))
        gpool = ctx.enter_context(tc.tile_pool(name="gpool", bufs=3))
        qpool = ctx.enter_context(tc.tile_pool(name="qpool", bufs=5))
        tpool = ctx.enter_context(tc.psum_pool(name="tpool", bufs=6))
        mpool = ctx.enter_context(tc.psum_pool(name="mpool", bufs=1))
        jpool = ctx.enter_context(tc.tile_pool(name="jpool", bufs=2))
        ctx.enter_context(tc.manual_schedule())

        x_tiles = {}

        def load(k):
            if k >= UNITS:
                return
            i0 = 2 * k
            xt = xin.tile([P, 2, DC * 512], BF16)
            if k in (0, UNITS - 1):
                for il in range(2):
                    nc.sync.dma_start(out=xt[:, il, :], in_=feature_map[i0 + il].rearrange("(p c) m -> p (c m)", c=DC))
            else:
                nc.sync.dma_start(
                    out=xt[:], in_=feature_map[i0 : i0 + 2].rearrange("i (p c) m -> p i (c m)", c=DC)
                )
            if k == UNITS - 1:
                nc.sync.dma_start(out=sc_bf[:], in_=scale.partition_broadcast(P))
            x_tiles[k] = xt

        def copy_words(on_scalar, dst, src):
            if on_scalar:
                nc.scalar.copy(out=dst, in_=src)
            else:
                nc.vector.tensor_copy(out=dst, in_=src)

        w_in = const.tile([P, 6, 512], BF16)
        nc.sync.dma_start(
            out=w_in[:],
            in_=weight2.rearrange("s q m -> (s q) m").rearrange("(j p) m -> p j m", p=P),
        )
        w_first = const.tile([P, 6 * P], F32)
        sc_bf = const.tile([P, 1], BF16)
        for k in range(X_BUFS):
            load(k)

        ident = const.tile([P, P], F32)
        make_identity(nc, ident[:])
        diffs = []
        for r in range(DIFF_BUFS):
            dt_r = const.tile([P, DC * P], F32, name="diff%d" % r)
            nc.gpsimd.memset(dt_r[:], 0.0)
            diffs.append(dt_r)

        warm = const.tile([P, 1], F32)
        nc.vector.memset(warm[:], 1.0)
        nc.scalar.activation(out=warm[:], in_=warm[:], func=ACT.Exp)

        w1c = const.tile([P, (NS + 2) * BLK], U32, align_bytes=64)
        w1s = const.tile([P, (NS + 2) * BLK], U8, align_bytes=64)
        w2c = const.tile([P, (NQ + 2) * BLK], U32, align_bytes=64)
        w2s = const.tile([P, (NQ + 2) * BLK], U8, align_bytes=64)
        c_sb = const.tile([P, DC * NQ * NS], F32)
        l2_sb = const.tile([P, P], F32)
        acc = const.tile([P, 2, 8], F32)
        sc_f = const.tile([P, 1], F32)
        cv = c_sb[:].rearrange("p (c k q i) -> p c k q i", c=DC, k=NS // 2, q=NQ, i=2)

        wg = []
        for r, slots in enumerate((16, 8, 16, 16)):
            wg_r = const.tile([P, slots * BLK * 4], BF16, align_bytes=64, name="wg%d" % r)
            wg.append(wg_r)
        wgv = [w[:].bitcast(F32).rearrange("p (l c u) -> p l c u", c=BLK, u=2) for w in wg]
        nc.vector.memset(w1c[:, NS * BLK :].bitcast(I32), 0)
        nc.vector.memset(w1s[:, NS * BLK :].bitcast(I32), 0)
        nc.vector.memset(wgv[2][:, :, NS:BLK, :], 0.0)
        nc.vector.memset(wgv[3][:, :, NS:BLK, :], 0.0)
        nc.vector.memset(w2c[:, NQ * BLK :].bitcast(I32), 0)
        nc.vector.memset(w2s[:, NQ * BLK :].bitcast(I32), 0)
        nc.vector.memset(l2_sb[:], 0.0)

        permuted = {}
        t_banks = {}
        grouped = {}
        quant = {}
        turned = {}

        def halves(words, chunks):
            return words.rearrange("p (c s j v e) -> p c s j v e", c=chunks, s=2, j=8, v=2, e=8)

        def gather(first, words, chunks):
            nc.vector.tensor_copy(
                out=first.rearrange("p (c j s e) -> p c s j e", c=chunks, s=2, j=8, e=8),
                in_=halves(words, chunks)[:, :, :, :, 0, :],
            )

        def fill(words, chunks):
            h = halves(words, chunks)
            nc.vector.tensor_copy(out=h[:, :, 1, :, 0, :], in_=h[:, :, 0, :, 1, :])

        def x_words(k):
            return x_tiles[k][:].rearrange("p i m -> p (i m)").bitcast(F32)

        def regroup(k, part, c0=0, c1=2 * DC):
            if k not in permuted:
                xp = ppool.tile([P, 2 * DC * P], F32)
                permuted[k] = xp
            words = x_words(k)[:, c0 * 256 : c1 * 256]
            if part == 0:
                gather(permuted[k][:, c0 * P : c1 * P], words, c1 - c0)
            else:
                fill(words, c1 - c0)

        def transposes(k):
            x32 = x_words(k)
            banks = []
            for b in range(DC):
                tb = tpool.tile([P, 512], F32, tag="tb")
                for g in (2 * b, 2 * b + 1):
                    for h in range(2):
                        src = x32[:, g * 256 + P : (g + 1) * 256] if h else permuted[k][:, g * P : (g + 1) * P]
                        at = (2 * (g - 2 * b) + h) * P
                        nc.tensor.transpose(tb[:, at : at + P], src, ident[:])
                banks.append(tb)
            t_banks[k] = banks
            g_tile = gpool.tile([P, 2 * DC * 512], BF16, align_bytes=64)
            grouped[k] = g_tile
            c_tile = qpool.tile([P, 2 * DC * P], U32, align_bytes=64)
            s_tile = qpool.tile([P, 2 * DC * P], U8, align_bytes=64)
            quant[k] = (c_tile, s_tile)

        def copy_bank(k, b, on_scalar):
            copy_words(
                on_scalar,
                grouped[k][:].bitcast(F32)[:, b * 512 : (b + 1) * 512].rearrange("p (c d h) -> p c d h", c=2, d=P, h=2),
                t_banks[k][b][:].rearrange("p (c h d) -> p c d h", c=2, h=2, d=P),
            )

        def quantise(k, g0, g1):
            codes, planes = quant[k]
            nc.vector.quantize_mx(
                out=codes[:, g0 * P : g1 * P].bitcast(FP8X4),
                scales=planes[:, g0 * P : g1 * P],
                in_=grouped[k][:, g0 * 512 : g1 * 512],
            )

        def mx_run(k, d0, d1, pool, tag):
            codes, planes = quant[k]
            wc, ws, w0 = (w2c, w2s, BLK * (2 * k - NS)) if 2 * k >= NS else (w1c, w1s, BLK * 2 * k)
            mb = pool.tile([P, 512], F32, tag=tag)
            for row in range(d1 - d0):
                for il in range(2):
                    g = il * DC + d0 + row
                    col = PAIR * row + BLK * il
                    width = P if col + P <= 512 else 2 * BLK
                    nc.tensor.matmul_mx(
                        out=mb[:, col : col + width],
                        lhsT=codes[:, g * P : (g + 1) * P].bitcast(FP8X4),
                        lhsT_scale=planes[:, g * P : (g + 1) * P],
                        rhs=wc[:, w0 : w0 + width].bitcast(FP8X4),
                        rhs_scale=ws[:, w0 : w0 + width],
                        start=True,
                        stop=True,
                    )
            return (k, d0, d1, mb)

        def drain(run):
            k, d0, d1, mb = run
            used = mb[:, 0 : (d1 - d0) * PAIR].rearrange("p (c j r) -> p c j r", j=3, r=BLK)[:, :, 0:3:2, :]
            if 2 * k >= NS:
                i0 = 2 * k - NS
                dv = diffs[i0 // 4 % DIFF_BUFS][:].rearrange("p (c i s) -> p c i s", c=DC, i=4, s=32)
                for il in range(2):
                    nc.vector.tensor_tensor(
                        out=dv[:, d0:d1, i0 % 4 + il, 0:NS].rearrange("p c (k i) -> p c k i", i=2),
                        in0=cv[:, d0:d1, :, i0 + il, :],
                        in1=used[:, :, il, 0:NS].rearrange("p c (k i) -> p c k i", i=2),
                        op=ALU.subtract,
                    )
            else:
                copy_words(
                    k in SDRAIN,
                    cv[:, d0:d1, k, :, :],
                    used.rearrange("p c i r -> p c r i"),
                )

        def turn_diffs(t, part, c0, c1):
            dt_ps = tpool.tile([P, 512], F32, tag="tb")
            for dc in range(c0, c1):
                nc.tensor.transpose(
                    dt_ps[:, (dc - c0) * P : (dc - c0 + 1) * P],
                    diffs[t % DIFF_BUFS][:, dc * P : (dc + 1) * P],
                    ident[:],
                )
            turned[(t, part)] = (dt_ps, (c1 - c0) * P)

        def square_sum(t, part):
            dt_ps, width = turned[(t, part)]
            junk = jpool.tile([P, 512], F32)
            nc.scalar.activation(
                out=junk[:, 0:width],
                in_=dt_ps[:, 0:width],
                func=ACT.Square,
                accum_out=acc[:, part, t : t + 1],
            )

        def turn_and_square(t):
            for part, (c0, c1) in enumerate(((0, 3), (3, DC))):
                turn_diffs(t, part, c0, c1)
                square_sum(t, part)

        w32 = w_in[:].rearrange("p j m -> p (j m)").bitcast(F32)
        gather(w_first[:], w32, 6)
        fill(w32, 6)
        for part in range(2):
            regroup(0, part, 0, DC)
        for b in range(3):
            wb = tpool.tile([P, 512], F32, tag="tb")
            for cl in range(2):
                for u in range(2):
                    nc.tensor.transpose(
                        wb[:, (2 * cl + u) * P : (2 * cl + u + 1) * P],
                        w32[:, (2 * b + cl) * 256 + P : (2 * b + cl + 1) * 256]
                        if u
                        else w_first[:, (2 * b + cl) * P : (2 * b + cl + 1) * P],
                        ident[:],
                    )
            on_scalar = b != 1
            wb_sq = wb[:].rearrange("p (c u s q) -> p c s q u", c=2, u=2, s=4, q=NQ)
            wb_qs = wb[:].rearrange("p (c u s q) -> p c q s u", c=2, u=2, s=4, q=NQ)
            for cl in range(2):
                j = 2 * b + cl
                s0 = 4 * j
                copy_words(on_scalar, wgv[s0 // 16][:, s0 % 16 : s0 % 16 + 4, 0:NQ, :], wb_sq[:, cl])
                for half in range(2):
                    copy_words(
                        on_scalar,
                        wgv[2 + half][:, :, s0 : s0 + 4, :],
                        wb_qs[:, cl, 16 * half : 16 * half + 16],
                    )
        for part in range(2):
            regroup(0, part, DC, 2 * DC)
        nc.vector.quantize_mx(out=w1c[:, 0:512].bitcast(FP8X4), scales=w1s[:, 0:512], in_=wg[0][:])
        nc.vector.quantize_mx(out=w1c[:, 512:768].bitcast(FP8X4), scales=w1s[:, 512:768], in_=wg[1][:])

        for part in range(2):
            regroup(1, part)
        runs = []
        to_turn = []
        for k in range(UNITS):
            ahead = 2 <= k + 2 < UNITS
            if k == UNITS - 1:
                quantise(k - 1, 0, 4)
                quantise(k - 1, 4, 8)
            elif k >= 1:
                quantise(k - 1, 0, 8)
            if ahead:
                regroup(k + 2, 0)
            turn_now = to_turn
            to_turn = []
            late = [run for run in runs if run[0] in SDRAIN]
            for run in runs:
                if run[0] not in SDRAIN:
                    drain(run)
                if 2 * run[0] >= NS and run[0] % 2 == 1:
                    to_turn.append((2 * run[0] - NS) // 4)
            runs = []
            if k >= 1:
                quantise(k - 1, 8, 10)
            if ahead:
                regroup(k + 2, 1)
            transposes(k)
            load(k + X_BUFS)
            if 2 <= k < 6:
                half, part = (k - 2) // 2, (k - 2) % 2
                col = 512 * half + 256 * part
                nc.vector.quantize_mx(
                    out=w2c[:, col : col + 256].bitcast(FP8X4),
                    scales=w2s[:, col : col + 256],
                    in_=wg[2 + half][:, 1024 * part : 1024 * (part + 1)],
                )
            for b in range(DC):
                copy_bank(k, b, b not in VCOPY.get(k, ()))
                if b == SD_AT:
                    for run in late:
                        drain(run)
            for t in turn_now:
                turn_and_square(t)
            if k >= 2:
                runs = [mx_run(k - 2, 0, DC, mpool, "m%d" % (k % 2))]

        for g0, g1 in ((0, 4), (4, 8), (8, 10)):
            quantise(27, g0, g1)
        runs.append(mx_run(26, 0, DC, tpool, "tb"))
        runs.append(mx_run(27, 0, 3, tpool, "tb"))
        runs.append(mx_run(27, 3, DC, tpool, "tb"))
        for run in runs:
            drain(run)
        turn_and_square(6)
        turn_and_square(7)
        nc.vector.tensor_scalar(out=sc_f[:], in0=sc_bf[:], scalar1=LOGIT_FACTOR, scalar2=None, op0=ALU.mult)
        part = const.tile([P, 8], F32)
        nc.vector.tensor_scalar(out=part[:], in0=acc[:, 0, :], scalar1=sc_f[:, 0:1], scalar2=None, op0=ALU.mult)
        nc.vector.scalar_tensor_tensor(
            out=l2_sb[:, 0:8], in0=acc[:, 1, :], scalar=sc_f[:, 0:1], in1=part[:], op0=ALU.mult, op1=ALU.add
        )
        fin = mpool.tile([P, 512], F32, tag="m1")
        nc.tensor.transpose(fin[:, 0:P], l2_sb[:], ident[:])
        z = fin[:, 0:P].rearrange("p (i s) -> p i s", i=4, s=32)[:, :, 0:NS]
        zs = const.tile([P, 4, NS], F32)
        ez = const.tile([P, 4, NS], F32)
        res = const.tile([P, 4, NS], F32)
        mx = const.tile([P, 4], F32)
        sm = const.tile([P, 4], F32)
        ls = const.tile([P, 4], F32)
        nc.vector.tensor_reduce(out=mx[:], in_=z, axis=AX.X, op=ALU.max)
        nc.vector.tensor_tensor(out=zs[:], in0=z, in1=mx[:].unsqueeze(2).to_broadcast([P, 4, NS]), op=ALU.subtract)
        nc.scalar.activation(out=ez[:], in_=zs[:], func=ACT.Exp)
        nc.vector.tensor_reduce(out=sm[:], in_=ez[:], axis=AX.X, op=ALU.add)
        nc.scalar.activation(out=ls[:], in_=sm[:], func=ACT.Ln)
        nc.vector.tensor_tensor(out=res[:], in0=zs[:], in1=ls[:].unsqueeze(2).to_broadcast([P, 4, NS]), op=ALU.subtract)
        nc.sync.dma_start(
            out=out.rearrange("(t l) s -> t (l s)", l=4),
            in_=res[0:8].rearrange("p l s -> p (l s)"),
        )
